import numpy as np
import ml_dtypes


def mxq(x, axis, fmt="e4m3"):
    dtype, down = {"e4m3": (ml_dtypes.float8_e4m3fn, 7), "e5m2": (ml_dtypes.float8_e5m2, 14)}[fmt]
    v = np.moveaxis(np.asarray(x, np.float32).astype(ml_dtypes.bfloat16).astype(np.float64), axis, -1)
    blocks = v.reshape(v.shape[:-1] + (-1, 32))
    amax = np.abs(blocks).max(-1, keepdims=True)
    byte = np.maximum(np.where(amax > 0, np.frexp(amax)[1] - 1 + 127, 0) - down, 1)
    scale = np.exp2(byte - 127.0)
    codes = (blocks / scale).astype(np.float32).astype(dtype).astype(np.float64)
    return np.moveaxis((codes * scale).reshape(v.shape), -1, axis)


WIDE = False


def mx_kscale(k):
    if not WIDE:
        return np.ones(k)
    levels = np.array([10, -10, 5, -5, 0])
    a = np.random.permutation(np.resize(levels, k // 512 * 4)).reshape(k // 512, 4)
    idx = np.arange(k)
    return np.exp2(a[idx // 512, idx % 128 // 32])


BF16 = ml_dtypes.bfloat16


def bf(x):
    return np.asarray(x, np.float32).astype(BF16)


def f64(x):
    return np.asarray(x).astype(np.float64)


E2M1 = np.array([0.0, 0.5, 1.0, 1.5, 2.0, 3.0, 4.0, 6.0, -0.0, -0.5, -1.0, -1.5, -2.0, -3.0, -4.0, -6.0])


def pack_weight(w, fmt):
    k, n = w.shape
    w = f64(bf(w)).reshape(k // 32, 32, n)
    amax = np.abs(w).max(1)
    if fmt == "e4m3":
        byte = np.frexp(amax)[1] - 1 + 127 - 7
    else:
        mant, ex = np.frexp(amax / 6.0)
        byte = np.where(mant > 0.5, ex, ex - 1) + 127
    byte = np.clip(np.where(amax > 0, byte, 1), 1, 254)
    scaled = (w * np.exp2(127.0 - byte)[:, None, :]).reshape(k, n).astype(np.float32)
    by_word = np.ascontiguousarray(scaled.reshape(k // 512, 128, 4, n).transpose(0, 1, 3, 2))
    if fmt == "e4m3":
        words = by_word.astype(ml_dtypes.float8_e4m3fn).view(np.uint8)
    else:
        c = by_word.astype(ml_dtypes.float4_e2m1fn).view(np.uint8) & 0xF
        words = c[..., 0::2] | (c[..., 1::2] << 4)
    return np.ascontiguousarray(words), np.ascontiguousarray(byte.astype(np.uint8).reshape(k // 512, 16, n))


def unpack_weight(words, scales, fmt):
    g, p, n, _ = words.shape
    if fmt == "e4m3":
        vals = np.ascontiguousarray(words).view(ml_dtypes.float8_e4m3fn).astype(np.float64)
    else:
        nib = np.empty((g, p, n, 4), np.uint8)
        nib[..., 0::2] = words & 0xF
        nib[..., 1::2] = words >> 4
        vals = E2M1[nib]
    vals = vals * np.repeat(np.exp2(scales.astype(np.float64) - 127.0), 8, axis=1)[..., None]
    return vals.transpose(0, 1, 3, 2).reshape(g * 512, n)


M, B, T, D, P = 3, 256, 8, 1024, 256
LN_EPS = 1e-5
NORM_EPS = 1e-12


def erf(v):
    a = np.clip(v, -6.0, 6.0)
    term = a.copy()
    total = a.copy()
    for n in range(1, 130):
        term = term * (2.0 * a * a / (2 * n + 1))
        total = total + term
    return 2.0 / np.sqrt(np.pi) * np.exp(-a * a) * total


def gelu_erf(v):
    return 0.5 * v * (1.0 + erf(v / np.sqrt(2.0)))


def setup_inputs():
    s = mx_kscale(D)
    feats = bf(np.random.standard_normal((M, B, T, D)) * s)
    w1 = np.random.standard_normal((M, D, D)) * np.sqrt(T / D) / s[None, :, None]
    b1 = bf(np.random.standard_normal((M, D)) * 0.3)
    w2 = np.random.standard_normal((M, D, P)) * 0.6 / np.sqrt(D)
    b2 = bf(0.25 + np.random.standard_normal((M, P)) * 0.15)
    gamma = bf(1.0 + np.random.standard_normal((M, P)) * 0.2)
    beta = bf(np.random.standard_normal((M, P)) * 0.3)
    w1_words, w1_scales = pack_weight(w1.reshape(-1, D), "e4m3")
    w2_words, w2_scales = pack_weight(w2.reshape(-1, P), "e4m3")
    return {"feats": feats,
            "W1_words": w1_words,
            "W1_scales": w1_scales,
            "b1": b1,
            "W2_words": w2_words,
            "W2_scales": w2_scales,
            "b2": b2,
            "gamma": gamma,
            "beta": beta}


def reference(feats, W1_words, W1_scales, b1, W2_words, W2_scales, b2, gamma, beta):
    pooled = f64(feats).mean(axis=2)
    h = gelu_erf((mxq(pooled, 2, "e4m3") @ unpack_weight(W1_words, W1_scales, "e4m3").reshape(M, D, D)) + f64(b1)[:, None, :])
    z = (mxq(h, 2, "e4m3") @ unpack_weight(W2_words, W2_scales, "e4m3").reshape(M, D, P)) + f64(b2)[:, None, :]
    mu = z.mean(axis=-1, keepdims=True)
    var = np.mean((z - mu) ** 2, axis=-1, keepdims=True)
    z = (z - mu) / np.sqrt(var + LN_EPS) * f64(gamma)[:, None, :] + f64(beta)[:, None, :]
    n = np.sqrt(np.sum(z * z, axis=-1, keepdims=True))
    return z / np.maximum(n, NORM_EPS)

@@ -1,0 +1,309 @@
+from contextlib import ExitStack
+
+import concourse.mybir as mybir
+from concourse.masks import make_identity
+
+BF16 = mybir.dt.bfloat16
+F32 = mybir.dt.float32
+I32 = mybir.dt.int32
+U32 = mybir.dt.uint32
+U8 = mybir.dt.uint8
+FP8X4 = mybir.dt.float8_e4m3fn_x4
+ACT = mybir.ActivationFunctionType
+ALU = mybir.AluOpType
+AXIS = mybir.AxisListType
+
+P = 128
+MODS, B, T, D, PROJ = 3, 256, 8, 1024, 256
+LN_EPS = 1e-5
+NORM_EPS = 1e-12
+
+PACK = 4
+K_PASS = P * PACK
+PASSES = D // K_PASS
+F_TILES = D // P
+PROJ_TILES = PROJ // P
+HALVES = B // P
+UNITS = MODS * HALVES
+GROUP_B = P // T
+CHUNK_B = 64
+GROUPS = CHUNK_B // GROUP_B
+CHUNKS = P // CHUNK_B
+SCALE_ROWS = 4
+
+FLOPS = 2 * MODS * B * D * (D + PROJ)
+
+
+def tile_semanticaligner_e_kernel(
+    tc, feats, w1_words, w1_scales, b1, w2_words, w2_scales, b2, gamma, beta, out
+):
+    nc = tc.nc
+    with ExitStack() as ctx:
+        const = ctx.enter_context(tc.tile_pool(name="const", bufs=1))
+        weights = ctx.enter_context(tc.tile_pool(name="weights", bufs=1))
+        loads = ctx.enter_context(tc.tile_pool(name="loads", bufs=UNITS * CHUNKS))
+        work = ctx.enter_context(tc.tile_pool(name="work", bufs=3))
+        small = ctx.enter_context(tc.tile_pool(name="small", bufs=3))
+        pool_psum = ctx.enter_context(tc.psum_pool(name="pool_psum", bufs=2))
+        turn_psum = ctx.enter_context(tc.psum_pool(name="turn_psum", bufs=3))
+        mx_psum = ctx.enter_context(tc.psum_pool(name="mx_psum", bufs=3))
+        ctx.enter_context(tc.manual_schedule())
+
+        vector_rows = const.tile([P, P], BF16)
+        nc.vector.memset(vector_rows[:], 0.0)
+        first_row = {}
+        next_row = 0
+        for name, vector in (("b1", b1), ("b2", b2), ("gamma", gamma), ("beta", beta)):
+            as_rows = vector.rearrange("m (c f) -> (m c) f", f=P)
+            first_row[name] = next_row
+            nc.scalar.dma_start(
+                out=vector_rows[next_row : next_row + as_rows.shape[0], :], in_=as_rows
+            )
+            next_row += as_rows.shape[0]
+
+        ident_bf = const.tile([P, P], BF16)
+        make_identity(nc, ident_bf[:])
+        ident_f32 = const.tile([P, P], F32)
+        make_identity(nc, ident_f32[:])
+
+        neg_half = const.tile([P, 1], F32)
+        nc.vector.memset(neg_half[:], -0.5)
+        warm = const.tile([P, 1], F32)
+        nc.scalar.activation(out=warm[:], in_=neg_half[:], func=ACT.Gelu)
+
+        selector_f32 = const.tile([P, GROUP_B], F32)
+        nc.vector.tensor_reduce(
+            out=selector_f32[:],
+            in_=ident_bf[:].rearrange("p (r t) -> p r t", t=T),
+            axis=AXIS.X,
+            op=ALU.add,
+        )
+        selector = const.tile([P, GROUP_B], BF16)
+        nc.vector.tensor_scalar(
+            out=selector[:], in0=selector_f32[:], scalar1=1.0 / T, scalar2=None, op0=ALU.mult
+        )
+
+        w1_planes = weights.tile([P, MODS * PASSES, D], U8, align_bytes=64)
+        nc.vector.memset(w1_planes[:].bitcast(I32), 0)
+        w2_planes = weights.tile([P, MODS * PASSES, PROJ], U8, align_bytes=64)
+        nc.vector.memset(w2_planes[:].bitcast(I32), 0)
+
+        w1_codes = weights.tile([P, MODS * PASSES, D], U32, align_bytes=64)
+        w2_codes = weights.tile([P, MODS * PASSES, PROJ], U32, align_bytes=64)
+        chunks = {}
+        for m in range(MODS):
+            for i in range(HALVES * CHUNKS):
+                chunk = loads.tile([P, GROUPS, D], BF16, tag="chunk")
+                nc.sync.dma_start(
+                    out=chunk[:],
+                    in_=feats[m, i * CHUNK_B : (i + 1) * CHUNK_B].rearrange(
+                        "(j r) t d -> (r t) j d", r=GROUP_B
+                    ),
+                )
+                chunks[(m * HALVES + i // CHUNKS, i % CHUNKS)] = chunk
+            if m == 0:
+                for planes, scales in ((w1_planes, w1_scales), (w2_planes, w2_scales)):
+                    by_row = scales.rearrange("g (q r) n -> r q g n", r=SCALE_ROWS)
+                    for r in range(SCALE_ROWS):
+                        nc.sync.dma_start(
+                            out=planes[r:P:32, :, :].bitcast(I32), in_=by_row[r].bitcast(I32)
+                        )
+            of_m = slice(m * PASSES, (m + 1) * PASSES)
+            for codes, words in ((w1_codes, w1_words), (w2_codes, w2_words)):
+                nc.sync.dma_start(
+                    out=codes[:, of_m, :].bitcast(I32),
+                    in_=words[of_m].rearrange("g p n t -> p g (n t)").bitcast(I32),
+                )
+
+        everywhere = {}
+        vector_cols = const.tile([P, P], BF16)
+
+        def turn_vectors():
+            cols_ps = turn_psum.tile([P, P], BF16, tag="turn")
+            nc.tensor.transpose(cols_ps[:], vector_rows[:], ident_bf[:])
+            nc.vector.tensor_copy(out=vector_cols[:], in_=cols_ps[:])
+
+        def spread(name, first, count):
+            bank = turn_psum.tile([P, count * P], BF16, tag="turn")
+            for i in range(count):
+                nc.tensor.transpose(
+                    bank[:, i * P : (i + 1) * P],
+                    vector_cols[:, first + i : first + i + 1].to_broadcast([P, P]),
+                    ident_bf[:],
+                )
+            everywhere[name] = const.tile([P, count * P], BF16, name=name)
+            nc.scalar.copy(out=everywhere[name][:], in_=bank[:])
+
+        tiles = {}
+
+        def pool(u, q):
+            if q == 0:
+                tiles["pooled", u] = work.tile(
+                    [P, PASSES, P, PACK], BF16, tag="pooled", name="pooled", align_bytes=64
+                )
+            mean_ps = pool_psum.tile([P, PASSES, CHUNK_B, PACK], F32, tag="mean")
+            for j in range(GROUPS):
+                rows = slice(j * GROUP_B, (j + 1) * GROUP_B)
+                for g in range(PASSES):
+                    for t in range(PACK):
+                        nc.tensor.matmul(
+                            out=mean_ps[:, g, rows, t],
+                            lhsT=chunks[u, q][:, j, g * K_PASS + t : (g + 1) * K_PASS : PACK],
+                            rhs=selector[:],
+                            start=True,
+                            stop=True,
+                        )
+            nc.scalar.copy(
+                out=tiles["pooled", u][:, :, q * CHUNK_B : (q + 1) * CHUNK_B, :], in_=mean_ps[:]
+            )
+
+        def quantise_pooled(u):
+            codes = work.tile([P, PASSES, P], U32, tag="pooled_codes", align_bytes=64)
+            planes = work.tile([P, PASSES, P], U8, tag="pooled_planes", align_bytes=64)
+            nc.vector.quantize_mx(
+                out=codes[:].rearrange("p g r -> p (g r)").bitcast(FP8X4),
+                scales=planes[:].rearrange("p g r -> p (g r)"),
+                in_=tiles["pooled", u][:].rearrange("p g r t -> p (g r t)"),
+            )
+            tiles["pooled_codes", u] = codes
+            tiles["pooled_planes", u] = planes
+
+        def first_matmul(u):
+            m = u // HALVES
+            pre = work.tile([P, PASSES, K_PASS], F32, tag="pre")
+            h_words = work.tile([P, PASSES, 2, P, 2], BF16, tag="h_words")
+            for n in range(PASSES):
+                cols = slice(n * K_PASS, (n + 1) * K_PASS)
+                acc = mx_psum.tile([P, K_PASS], F32, tag="acc")
+                for g in range(PASSES):
+                    nc.tensor.matmul_mx(
+                        out=acc[:],
+                        lhsT=tiles["pooled_codes", u][:, g, :].bitcast(FP8X4),
+                        lhsT_scale=tiles["pooled_planes", u][:, g, :],
+                        rhs=w1_codes[:, m * PASSES + g, cols].bitcast(FP8X4),
+                        rhs_scale=w1_planes[:, m * PASSES + g, cols],
+                        start=(g == 0),
+                        stop=(g == PASSES - 1),
+                    )
+                nc.vector.tensor_tensor(
+                    out=pre[:, n, :], in0=acc[:], in1=everywhere["b1_%d" % m][:, cols], op=ALU.add
+                )
+                nc.scalar.activation(
+                    out=h_words[:, n],
+                    in_=pre[:, n, :].rearrange("r (p s e) -> r s p e", s=2, e=2),
+                    func=ACT.Gelu,
+                )
+            tiles["h_words", u] = h_words
+
+        def quantise_h(u):
+            grouped = work.tile([P, PASSES, P, PACK], BF16, tag="h_grouped", align_bytes=64)
+            codes = work.tile([P, PASSES, P], U32, tag="h_codes", align_bytes=64)
+            planes = work.tile([P, PASSES, P], U8, tag="h_planes", align_bytes=64)
+            for n in range(PASSES):
+                word_ps = turn_psum.tile([P, 2, P], F32, tag="turn")
+                for s in range(2):
+                    nc.tensor.transpose(
+                        word_ps[:, s, :],
+                        tiles["h_words", u][:, n, s].rearrange("r p e -> r (p e)").bitcast(F32),
+                        ident_f32[:],
+                    )
+                nc.scalar.copy(
+                    out=grouped[:, n].bitcast(F32), in_=word_ps[:].rearrange("p s r -> p r s")
+                )
+            for n in range(PASSES):
+                nc.vector.quantize_mx(
+                    out=codes[:, n, :].bitcast(FP8X4),
+                    scales=planes[:, n, :],
+                    in_=grouped[:, n].rearrange("p r t -> p (r t)"),
+                )
+            tiles["h_codes", u] = codes
+            tiles["h_planes", u] = planes
+
+        def second_matmul(u):
+            m = u // HALVES
+            of_m = slice(m * PROJ, (m + 1) * PROJ)
+            z_ps = mx_psum.tile([P, PROJ], F32, tag="acc")
+            for g in range(PASSES):
+                nc.tensor.matmul_mx(
+                    out=z_ps[:],
+                    lhsT=tiles["h_codes", u][:, g, :].bitcast(FP8X4),
+                    lhsT_scale=tiles["h_planes", u][:, g, :],
+                    rhs=w2_codes[:, m * PASSES + g, :].bitcast(FP8X4),
+                    rhs_scale=w2_planes[:, m * PASSES + g, :],
+                    start=(g == 0),
+                    stop=(g == PASSES - 1),
+                )
+            z = work.tile([P, PROJ], F32, tag="z")
+            nc.vector.tensor_tensor(out=z[:], in0=z_ps[:], in1=everywhere["b2"][:, of_m], op=ALU.add)
+            stats = small.tile([P, 6], F32, tag="stats")
+            nc.vector.bn_stats(out=stats[:], in_=z[:])
+            mean_var = small.tile([P, 2], F32, tag="mean_var")
+            nc.vector.bn_aggr(out=mean_var[:], in_=stats[:])
+            var_eps = small.tile([P, 1], F32, tag="var_eps")
+            nc.gpsimd.tensor_scalar(
+                out=var_eps[:], in0=mean_var[:, 1:2], scalar1=LN_EPS, scalar2=None, op0=ALU.add
+            )
+            rstd = small.tile([P, 1], F32, tag="rstd")
+            nc.gpsimd.tensor_tensor(out=rstd[:], in0=var_eps[:], in1=neg_half[:], op=ALU.pow)
+            centred = work.tile([P, PROJ], F32, tag="centred")
+            nc.vector.scalar_tensor_tensor(
+                out=centred[:],
+                in0=z[:],
+                scalar=mean_var[:, 0:1],
+                in1=everywhere["gamma"][:, of_m],
+                op0=ALU.subtract,
+                op1=ALU.mult,
+            )
+            y = work.tile([P, PROJ], F32, tag="y")
+            nc.vector.scalar_tensor_tensor(
+                out=y[:],
+                in0=centred[:],
+                scalar=rstd[:],
+                in1=everywhere["beta"][:, of_m],
+                op0=ALU.mult,
+                op1=ALU.add,
+            )
+            tiles["y", u] = y
+
+        def inverse_norm(u):
+            squares = work.tile([P, PROJ], F32, tag="squares")
+            sum_sq = small.tile([P, 1], F32, tag="sum_sq")
+            nc.scalar.activation(
+                out=squares[:], in_=tiles["y", u][:], func=ACT.Square, accum_out=sum_sq[:]
+            )
+            floored = small.tile([P, 1], F32, tag="floored")
+            nc.gpsimd.tensor_scalar(
+                out=floored[:], in0=sum_sq[:], scalar1=NORM_EPS * NORM_EPS, scalar2=None, op0=ALU.max
+            )
+            rnorm = small.tile([P, 1], F32, tag="rnorm")
+            nc.gpsimd.tensor_tensor(out=rnorm[:], in0=floored[:], in1=neg_half[:], op=ALU.pow)
+            tiles["rnorm", u] = rnorm
+
+        def finish(u):
+            m, half = divmod(u, HALVES)
+            result = work.tile([P, PROJ], F32, tag="result")
+            nc.scalar.activation(
+                out=result[:], in_=tiles["y", u][:], func=ACT.Copy, scale=tiles["rnorm", u][:]
+            )
+            nc.sync.dma_start(out=out[m, half * P : (half + 1) * P, :], in_=result[:])
+
+        def stage(work_of, u):
+            if 0 <= u < UNITS:
+                work_of(u)
+
+        for step in range(UNITS + 3):
+            stage(lambda u: pool(u, 0), step)
+            if step == 0:
+                turn_vectors()
+            if step < UNITS and step % HALVES == 0:
+                spread("b1_%d" % (step // HALVES), first_row["b1"] + (step // HALVES) * F_TILES, F_TILES)
+            stage(finish, step - 3)
+            stage(first_matmul, step - 1)
+            stage(second_matmul, step - 2)
+            stage(lambda u: pool(u, 1), step)
+            stage(quantise_pooled, step)
+            if step == 0:
+                for name in ("b2", "gamma", "beta"):
+                    spread(name, first_row[name], MODS * PROJ_TILES)
+            stage(quantise_h, step - 1)
+            stage(inverse_norm, step - 2)

@@ -26,7 +26,7 @@ PROJ_TILES = PROJ // P
 HALVES = B // P
 UNITS = MODS * HALVES
 GROUP_B = P // T
-CHUNK_B = 64
+CHUNK_B = 32
 GROUPS = CHUNK_B // GROUP_B
 CHUNKS = P // CHUNK_B
 SCALE_ROWS = 4
@@ -43,11 +43,17 @@ def tile_semanticaligner_e_kernel(
         weights = ctx.enter_context(tc.tile_pool(name="weights", bufs=1))
         loads = ctx.enter_context(tc.tile_pool(name="loads", bufs=UNITS * CHUNKS))
         work = ctx.enter_context(tc.tile_pool(name="work", bufs=3))
+        results = ctx.enter_context(tc.tile_pool(name="results", bufs=UNITS))
         small = ctx.enter_context(tc.tile_pool(name="small", bufs=3))
-        pool_psum = ctx.enter_context(tc.psum_pool(name="pool_psum", bufs=2))
-        turn_psum = ctx.enter_context(tc.psum_pool(name="turn_psum", bufs=3))
+        pool_psum = ctx.enter_context(tc.psum_pool(name="pool_psum", bufs=3))
+        turn_psum = ctx.enter_context(tc.psum_pool(name="turn_psum", bufs=2))
         mx_psum = ctx.enter_context(tc.psum_pool(name="mx_psum", bufs=3))
         ctx.enter_context(tc.manual_schedule())
+
+        w1_planes = weights.tile([P, MODS * PASSES, D], U8, align_bytes=64)
+        nc.vector.memset(w1_planes[:].bitcast(I32), 0)
+        w2_planes = weights.tile([P, MODS * PASSES, PROJ], U8, align_bytes=64)
+        nc.vector.memset(w2_planes[:].bitcast(I32), 0)
 
         vector_rows = const.tile([P, P], BF16)
         nc.vector.memset(vector_rows[:], 0.0)
@@ -83,14 +89,27 @@ def tile_semanticaligner_e_kernel(
             out=selector[:], in0=selector_f32[:], scalar1=1.0 / T, scalar2=None, op0=ALU.mult
         )
 
-        w1_planes = weights.tile([P, MODS * PASSES, D], U8, align_bytes=64)
-        nc.vector.memset(w1_planes[:].bitcast(I32), 0)
-        w2_planes = weights.tile([P, MODS * PASSES, PROJ], U8, align_bytes=64)
-        nc.vector.memset(w2_planes[:].bitcast(I32), 0)
-
         w1_codes = weights.tile([P, MODS * PASSES, D], U32, align_bytes=64)
         w2_codes = weights.tile([P, MODS * PASSES, PROJ], U32, align_bytes=64)
         chunks = {}
+        def load_scales():
+            for planes, scales in ((w1_planes, w1_scales), (w2_planes, w2_scales)):
+                by_row = scales.rearrange("g (q r) n -> r q g n", r=SCALE_ROWS)
+                for r in range(SCALE_ROWS):
+                    nc.sync.dma_start(
+                        out=planes[r:P:32, :, :].bitcast(I32), in_=by_row[r].bitcast(I32)
+                    )
+
+        pieces = [(w1_codes, w1_words, g, g + 1) for g in range(PASSES)]
+        pieces.append((w2_codes, w2_words, 0, PASSES))
+
+        def load_piece(m, codes, words, first, end):
+            of_m = slice(m * PASSES + first, m * PASSES + end)
+            nc.sync.dma_start(
+                out=codes[:, of_m, :].bitcast(I32),
+                in_=words[of_m].rearrange("g p n t -> p g (n t)").bitcast(I32),
+            )
+
         for m in range(MODS):
             for i in range(HALVES * CHUNKS):
                 chunk = loads.tile([P, GROUPS, D], BF16, tag="chunk")
@@ -101,19 +120,10 @@ def tile_semanticaligner_e_kernel(
                     ),
                 )
                 chunks[(m * HALVES + i // CHUNKS, i % CHUNKS)] = chunk
-            if m == 0:
-                for planes, scales in ((w1_planes, w1_scales), (w2_planes, w2_scales)):
-                    by_row = scales.rearrange("g (q r) n -> r q g n", r=SCALE_ROWS)
-                    for r in range(SCALE_ROWS):
-                        nc.sync.dma_start(
-                            out=planes[r:P:32, :, :].bitcast(I32), in_=by_row[r].bitcast(I32)
-                        )
-            of_m = slice(m * PASSES, (m + 1) * PASSES)
-            for codes, words in ((w1_codes, w1_words), (w2_codes, w2_words)):
-                nc.sync.dma_start(
-                    out=codes[:, of_m, :].bitcast(I32),
-                    in_=words[of_m].rearrange("g p n t -> p g (n t)").bitcast(I32),
-                )
+                if (m, i) == (0, CHUNKS - 1):
+                    load_scales()
+                if CHUNKS - 1 <= i < CHUNKS - 1 + len(pieces):
+                    load_piece(m, *pieces[i - CHUNKS + 1])
 
         everywhere = {}
         vector_cols = const.tile([P, P], BF16)
@@ -141,20 +151,24 @@ def tile_semanticaligner_e_kernel(
                 tiles["pooled", u] = work.tile(
                     [P, PASSES, P, PACK], BF16, tag="pooled", name="pooled", align_bytes=64
                 )
-            mean_ps = pool_psum.tile([P, PASSES, CHUNK_B, PACK], F32, tag="mean")
+            mean_ps = pool_psum.tile([P, PASSES, PACK, CHUNK_B], F32, tag="mean")
             for j in range(GROUPS):
                 rows = slice(j * GROUP_B, (j + 1) * GROUP_B)
                 for g in range(PASSES):
                     for t in range(PACK):
                         nc.tensor.matmul(
-                            out=mean_ps[:, g, rows, t],
+                            out=mean_ps[:, g, t, rows],
                             lhsT=chunks[u, q][:, j, g * K_PASS + t : (g + 1) * K_PASS : PACK],
                             rhs=selector[:],
                             start=True,
                             stop=True,
                         )
+            tiles["mean_ps", u, q] = mean_ps
+
+        def round_mean(u, q):
             nc.scalar.copy(
-                out=tiles["pooled", u][:, :, q * CHUNK_B : (q + 1) * CHUNK_B, :], in_=mean_ps[:]
+                out=tiles["pooled", u][:, :, q * CHUNK_B : (q + 1) * CHUNK_B, :],
+                in_=tiles["mean_ps", u, q][:].rearrange("p g t r -> p g r t"),
             )
 
         def quantise_pooled(u):
@@ -168,73 +182,93 @@ def tile_semanticaligner_e_kernel(
             tiles["pooled_codes", u] = codes
             tiles["pooled_planes", u] = planes
 
-        def first_matmul(u):
+        def first_matmul(u, n):
             m = u // HALVES
-            pre = work.tile([P, PASSES, K_PASS], F32, tag="pre")
-            h_words = work.tile([P, PASSES, 2, P, 2], BF16, tag="h_words")
-            for n in range(PASSES):
-                cols = slice(n * K_PASS, (n + 1) * K_PASS)
-                acc = mx_psum.tile([P, K_PASS], F32, tag="acc")
-                for g in range(PASSES):
-                    nc.tensor.matmul_mx(
-                        out=acc[:],
-                        lhsT=tiles["pooled_codes", u][:, g, :].bitcast(FP8X4),
-                        lhsT_scale=tiles["pooled_planes", u][:, g, :],
-                        rhs=w1_codes[:, m * PASSES + g, cols].bitcast(FP8X4),
-                        rhs_scale=w1_planes[:, m * PASSES + g, cols],
-                        start=(g == 0),
-                        stop=(g == PASSES - 1),
-                    )
-                nc.vector.tensor_tensor(
-                    out=pre[:, n, :], in0=acc[:], in1=everywhere["b1_%d" % m][:, cols], op=ALU.add
+            cols = slice(n * K_PASS, (n + 1) * K_PASS)
+            acc = mx_psum.tile([P, K_PASS], F32, tag="acc")
+            for g in range(PASSES):
+                nc.tensor.matmul_mx(
+                    out=acc[:],
+                    lhsT=tiles["pooled_codes", u][:, g, :].bitcast(FP8X4),
+                    lhsT_scale=tiles["pooled_planes", u][:, g, :],
+                    rhs=w1_codes[:, m * PASSES + g, cols].bitcast(FP8X4),
+                    rhs_scale=w1_planes[:, m * PASSES + g, cols],
+                    start=(g == 0),
+                    stop=(g == PASSES - 1),
                 )
-                nc.scalar.activation(
-                    out=h_words[:, n],
-                    in_=pre[:, n, :].rearrange("r (p s e) -> r s p e", s=2, e=2),
-                    func=ACT.Gelu,
-                )
-            tiles["h_words", u] = h_words
+            tiles["acc", u, n] = acc
 
-        def quantise_h(u):
-            grouped = work.tile([P, PASSES, P, PACK], BF16, tag="h_grouped", align_bytes=64)
-            codes = work.tile([P, PASSES, P], U32, tag="h_codes", align_bytes=64)
-            planes = work.tile([P, PASSES, P], U8, tag="h_planes", align_bytes=64)
-            for n in range(PASSES):
-                word_ps = turn_psum.tile([P, 2, P], F32, tag="turn")
-                for s in range(2):
-                    nc.tensor.transpose(
-                        word_ps[:, s, :],
-                        tiles["h_words", u][:, n, s].rearrange("r p e -> r (p e)").bitcast(F32),
-                        ident_f32[:],
-                    )
-                nc.scalar.copy(
-                    out=grouped[:, n].bitcast(F32), in_=word_ps[:].rearrange("p s r -> p r s")
+        def add_bias(u, n):
+            cols = slice(n * K_PASS, (n + 1) * K_PASS)
+            pre = work.tile([P, K_PASS], F32, tag="pre")
+            nc.vector.tensor_tensor(
+                out=pre[:],
+                in0=tiles["acc", u, n][:],
+                in1=everywhere["b1_%d" % (u // HALVES)][:, cols],
+                op=ALU.add,
+            )
+            tiles["pre", u, n] = pre
+
+        def gelu(u, n):
+            h_words = work.tile([P, 2, P, 2], BF16, tag="h_words")
+            nc.scalar.activation(
+                out=h_words[:],
+                in_=tiles["pre", u, n][:].rearrange("r (p s e) -> r s p e", s=2, e=2),
+                func=ACT.Gelu,
+            )
+            tiles["h_words", u, n] = h_words
+
+        def turn_h(u, n):
+            word_ps = turn_psum.tile([P, 2, P], F32, tag="turn")
+            for s in range(2):
+                nc.tensor.transpose(
+                    word_ps[:, s, :],
+                    tiles["h_words", u, n][:, s].rearrange("r p e -> r (p e)").bitcast(F32),
+                    ident_f32[:],
                 )
-            for n in range(PASSES):
-                nc.vector.quantize_mx(
-                    out=codes[:, n, :].bitcast(FP8X4),
-                    scales=planes[:, n, :],
-                    in_=grouped[:, n].rearrange("p r t -> p (r t)"),
-                )
-            tiles["h_codes", u] = codes
-            tiles["h_planes", u] = planes
+            tiles["word_ps", u, n] = word_ps
+
+        def group_h(u, n):
+            grouped = work.tile([P, P, PACK], BF16, tag="h_grouped", align_bytes=64)
+            nc.scalar.copy(
+                out=grouped[:].bitcast(F32),
+                in_=tiles["word_ps", u, n][:].rearrange("p s r -> p r s"),
+            )
+            tiles["grouped", u, n] = grouped
+
+        def quantise_h(u, n):
+            codes = work.tile([P, P], U32, tag="h_codes%d" % n, name="h_codes", align_bytes=64)
+            planes = work.tile([P, P], U8, tag="h_planes%d" % n, name="h_planes", align_bytes=64)
+            nc.vector.quantize_mx(
+                out=codes[:].bitcast(FP8X4),
+                scales=planes[:],
+                in_=tiles["grouped", u, n][:].rearrange("p r t -> p (r t)"),
+            )
+            tiles["h_codes", u, n] = codes
+            tiles["h_planes", u, n] = planes
 
         def second_matmul(u):
             m = u // HALVES
-            of_m = slice(m * PROJ, (m + 1) * PROJ)
             z_ps = mx_psum.tile([P, PROJ], F32, tag="acc")
             for g in range(PASSES):
                 nc.tensor.matmul_mx(
                     out=z_ps[:],
-                    lhsT=tiles["h_codes", u][:, g, :].bitcast(FP8X4),
-                    lhsT_scale=tiles["h_planes", u][:, g, :],
+                    lhsT=tiles["h_codes", u, g][:].bitcast(FP8X4),
+                    lhsT_scale=tiles["h_planes", u, g][:],
                     rhs=w2_codes[:, m * PASSES + g, :].bitcast(FP8X4),
                     rhs_scale=w2_planes[:, m * PASSES + g, :],
                     start=(g == 0),
                     stop=(g == PASSES - 1),
                 )
+            tiles["z_ps", u] = z_ps
+
+        def centre(u):
+            m = u // HALVES
+            of_m = slice(m * PROJ, (m + 1) * PROJ)
             z = work.tile([P, PROJ], F32, tag="z")
-            nc.vector.tensor_tensor(out=z[:], in0=z_ps[:], in1=everywhere["b2"][:, of_m], op=ALU.add)
+            nc.vector.tensor_tensor(
+                out=z[:], in0=tiles["z_ps", u][:], in1=everywhere["b2"][:, of_m], op=ALU.add
+            )
             stats = small.tile([P, 6], F32, tag="stats")
             nc.vector.bn_stats(out=stats[:], in_=z[:])
             mean_var = small.tile([P, 2], F32, tag="mean_var")
@@ -254,12 +288,17 @@ def tile_semanticaligner_e_kernel(
                 op0=ALU.subtract,
                 op1=ALU.mult,
             )
+            tiles["centred", u] = centred
+            tiles["rstd", u] = rstd
+
+        def normalise(u):
+            m = u // HALVES
             y = work.tile([P, PROJ], F32, tag="y")
             nc.vector.scalar_tensor_tensor(
                 out=y[:],
-                in0=centred[:],
-                scalar=rstd[:],
-                in1=everywhere["beta"][:, of_m],
+                in0=tiles["centred", u][:],
+                scalar=tiles["rstd", u][:],
+                in1=everywhere["beta"][:, m * PROJ : (m + 1) * PROJ],
                 op0=ALU.mult,
                 op1=ALU.add,
             )
@@ -280,30 +319,81 @@ def tile_semanticaligner_e_kernel(
             tiles["rnorm", u] = rnorm
 
         def finish(u):
-            m, half = divmod(u, HALVES)
-            result = work.tile([P, PROJ], F32, tag="result")
+            result = results.tile([P, PROJ], F32, tag="result")
             nc.scalar.activation(
                 out=result[:], in_=tiles["y", u][:], func=ACT.Copy, scale=tiles["rnorm", u][:]
             )
-            nc.sync.dma_start(out=out[m, half * P : (half + 1) * P, :], in_=result[:])
+            tiles["result", u] = result
 
-        def stage(work_of, u):
+        def store(queue, u):
+            m, half = divmod(u, HALVES)
+            queue.dma_start(out=out[m, half * P : (half + 1) * P, :], in_=tiles["result", u][:])
+
+        def stage(work_of, u, *rest):
             if 0 <= u < UNITS:
-                work_of(u)
+                work_of(u, *rest)
 
-        for step in range(UNITS + 3):
-            stage(lambda u: pool(u, 0), step)
-            if step == 0:
+        def both(work_of, u):
+            if 0 <= u < UNITS:
+                for n in range(PASSES):
+                    work_of(u, n)
+
+        for u in range(UNITS):
+            m, half = divmod(u, HALVES)
+            pool(u, 0)
+            round_mean(u, 0)
+            both(turn_h, u - 2)
+            stage(normalise, u - 3)
+            stage(inverse_norm, u - 3)
+            both(group_h, u - 2)
+            both(quantise_h, u - 2)
+            pool(u, 1)
+            round_mean(u, 1)
+            stage(finish, u - 3)
+            if u == 0:
                 turn_vectors()
-            if step < UNITS and step % HALVES == 0:
-                spread("b1_%d" % (step // HALVES), first_row["b1"] + (step // HALVES) * F_TILES, F_TILES)
-            stage(finish, step - 3)
-            stage(first_matmul, step - 1)
-            stage(second_matmul, step - 2)
-            stage(lambda u: pool(u, 1), step)
-            stage(quantise_pooled, step)
-            if step == 0:
+            both(first_matmul, u - 1)
+            both(add_bias, u - 1)
+            stage(gelu, u - 1, 0)
+            pool(u, 2)
+            round_mean(u, 2)
+            stage(gelu, u - 1, 1)
+            if half == 0:
+                spread("b1_%d" % m, first_row["b1"] + m * F_TILES, F_TILES)
+            stage(second_matmul, u - 2)
+            stage(centre, u - 2)
+            pool(u, 3)
+            round_mean(u, 3)
+            if u == 0:
                 for name in ("b2", "gamma", "beta"):
                     spread(name, first_row[name], MODS * PROJ_TILES)
-            stage(quantise_h, step - 1)
-            stage(inverse_norm, step - 2)
+            quantise_pooled(u)
+
+        last = UNITS - 1
+        both(turn_h, last - 1)
+        both(group_h, last - 1)
+        both(quantise_h, last - 1)
+        normalise(last - 2)
+        for u in range(last - 2):
+            store(nc.scalar, u)
+        both(first_matmul, last)
+        both(add_bias, last)
+        both(gelu, last)
+        inverse_norm(last - 2)
+        second_matmul(last - 1)
+        centre(last - 1)
+        both(turn_h, last)
+        both(group_h, last)
+        both(quantise_h, last)
+        finish(last - 2)
+        store(nc.sync, last - 2)
+        normalise(last - 1)
+        second_matmul(last)
+        centre(last)
+        inverse_norm(last - 1)
+        normalise(last)
+        inverse_norm(last)
+        finish(last - 1)
+        store(nc.sync, last - 1)
+        finish(last)
+        store(nc.sync, last)

@@ -151,7 +151,18 @@ def tile_semanticaligner_e_kernel(
                 tiles["pooled", u] = work.tile(
                     [P, PASSES, P, PACK], BF16, tag="pooled", name="pooled", align_bytes=64
                 )
-            mean_ps = pool_psum.tile([P, PASSES, PACK, CHUNK_B], F32, tag="mean")
+            bank = pool_psum.tile([P, 2, PASSES * PACK * CHUNK_B], F32, tag="mean")
+            if u >= 2:
+                nc.tensor.matmul_mx(
+                    out=bank[:, 1, :],
+                    lhsT=tiles["pooled_codes", u - 2][:, 0, :].bitcast(FP8X4),
+                    lhsT_scale=tiles["pooled_planes", u - 2][:, 0, :],
+                    rhs=w1_codes[:, 0, : bank.shape[2]].bitcast(FP8X4),
+                    rhs_scale=w1_planes[:, 0, : bank.shape[2]],
+                    start=True,
+                    stop=True,
+                )
+            mean_ps = bank[:, 0, :].rearrange("p (g t r) -> p g t r", g=PASSES, t=PACK)
             for j in range(GROUPS):
                 rows = slice(j * GROUP_B, (j + 1) * GROUP_B)
                 for g in range(PASSES):
@@ -168,7 +179,7 @@ def tile_semanticaligner_e_kernel(
         def round_mean(u, q):
             nc.scalar.copy(
                 out=tiles["pooled", u][:, :, q * CHUNK_B : (q + 1) * CHUNK_B, :],
-                in_=tiles["mean_ps", u, q][:].rearrange("p g t r -> p g r t"),
+                in_=tiles["mean_ps", u, q].rearrange("p g t r -> p g r t"),
             )
 
         def quantise_pooled(u):

@@ -29,7 +29,9 @@ GROUP_B = P // T
 CHUNK_B = 32
 GROUPS = CHUNK_B // GROUP_B
 CHUNKS = P // CHUNK_B
+QUADRANT = 32
 SCALE_ROWS = 4
+PLANES = 4
 
 FLOPS = 2 * MODS * B * D * (D + PROJ)
 
@@ -50,10 +52,16 @@ def tile_semanticaligner_e_kernel(
         mx_psum = ctx.enter_context(tc.psum_pool(name="mx_psum", bufs=3))
         ctx.enter_context(tc.manual_schedule())
 
-        w1_planes = weights.tile([P, MODS * PASSES, D], U8, align_bytes=64)
-        nc.vector.memset(w1_planes[:].bitcast(I32), 0)
+        w1_planes = []
+        for first in range(0, MODS * PASSES, PLANES):
+            shared = weights.tile([P, D], U8, name="w1_planes%d" % first, align_bytes=64)
+            nc.vector.memset(shared[:].bitcast(I32), 0)
+            w1_planes.append(shared)
         w2_planes = weights.tile([P, MODS * PASSES, PROJ], U8, align_bytes=64)
         nc.vector.memset(w2_planes[:].bitcast(I32), 0)
+
+        def w1_plane(i, cols):
+            return w1_planes[i // PLANES][i % PLANES * SCALE_ROWS :, cols]
 
         vector_rows = const.tile([P, P], BF16)
         nc.vector.memset(vector_rows[:], 0.0)
@@ -92,38 +100,56 @@ def tile_semanticaligner_e_kernel(
         w1_codes = weights.tile([P, MODS * PASSES, D], U32, align_bytes=64)
         w2_codes = weights.tile([P, MODS * PASSES, PROJ], U32, align_bytes=64)
         chunks = {}
-        def load_scales():
-            for planes, scales in ((w1_planes, w1_scales), (w2_planes, w2_scales)):
-                by_row = scales.rearrange("g (q r) n -> r q g n", r=SCALE_ROWS)
-                for r in range(SCALE_ROWS):
-                    nc.sync.dma_start(
-                        out=planes[r:P:32, :, :].bitcast(I32), in_=by_row[r].bitcast(I32)
-                    )
-
-        pieces = [(w1_codes, w1_words, g, g + 1) for g in range(PASSES)]
-        pieces.append((w2_codes, w2_words, 0, PASSES))
-
-        def load_piece(m, codes, words, first, end):
-            of_m = slice(m * PASSES + first, m * PASSES + end)
+        def load_w1_scales(first, quadrant):
+            passes = min(PLANES, MODS * PASSES - first)
+            rows = slice(quadrant * SCALE_ROWS, (quadrant + 1) * SCALE_ROWS)
+            start = quadrant * QUADRANT
             nc.sync.dma_start(
-                out=codes[:, of_m, :].bitcast(I32),
-                in_=words[of_m].rearrange("g p n t -> p g (n t)").bitcast(I32),
+                out=w1_planes[first // PLANES][start : start + passes * SCALE_ROWS, :].bitcast(I32),
+                in_=w1_scales[first : first + passes, rows, :].bitcast(I32),
             )
 
+        def load_w2_scales(r):
+            nc.sync.dma_start(
+                out=w2_planes[r:P:QUADRANT, :, :].bitcast(I32),
+                in_=w2_scales.rearrange("g (q r) n -> r q g n", r=SCALE_ROWS)[r].bitcast(I32),
+            )
+
+        def load_weights(codes, words, first, end):
+            nc.sync.dma_start(
+                out=codes[:, first:end, :].bitcast(I32),
+                in_=words[first:end].rearrange("g p n t -> p g (n t)").bitcast(I32),
+            )
+
+        def load_chunk(u, c):
+            m, half = divmod(u, HALVES)
+            first = half * P + c * CHUNK_B
+            chunk = loads.tile([P, GROUPS, D], BF16, tag="chunk")
+            nc.sync.dma_start(
+                out=chunk[:],
+                in_=feats[m, first : first + CHUNK_B].rearrange("(j r) t d -> (r t) j d", r=GROUP_B),
+            )
+            chunks[u, c] = chunk
+
+        scale_loads = [(load_w1_scales, 0, q) for q in range(P // QUADRANT)]
+        scale_loads += [(load_w2_scales, r) for r in range(SCALE_ROWS)]
+        scale_loads += [(load_w1_scales, PLANES, q) for q in range(P // QUADRANT)]
+
+        def load_some_scales(count):
+            for load, *args in scale_loads[:count]:
+                load(*args)
+            scale_loads[:count] = []
+
         for m in range(MODS):
+            of_m = m * PASSES
+            pieces = [(w1_codes, w1_words, of_m + g, of_m + g + 1) for g in range(PASSES)]
+            pieces.append((w2_codes, w2_words, of_m, of_m + PASSES))
             for i in range(HALVES * CHUNKS):
-                chunk = loads.tile([P, GROUPS, D], BF16, tag="chunk")
-                nc.sync.dma_start(
-                    out=chunk[:],
-                    in_=feats[m, i * CHUNK_B : (i + 1) * CHUNK_B].rearrange(
-                        "(j r) t d -> (r t) j d", r=GROUP_B
-                    ),
-                )
-                chunks[(m * HALVES + i // CHUNKS, i % CHUNKS)] = chunk
-                if (m, i) == (0, CHUNKS - 1):
-                    load_scales()
+                load_chunk(m * HALVES + i // CHUNKS, i % CHUNKS)
+                if i >= 2:
+                    load_some_scales(2)
                 if CHUNKS - 1 <= i < CHUNKS - 1 + len(pieces):
-                    load_piece(m, *pieces[i - CHUNKS + 1])
+                    load_weights(*pieces[i - CHUNKS + 1])
 
         everywhere = {}
         vector_cols = const.tile([P, P], BF16)
@@ -158,7 +184,7 @@ def tile_semanticaligner_e_kernel(
                     lhsT=tiles["pooled_codes", u - 2][:, 0, :].bitcast(FP8X4),
                     lhsT_scale=tiles["pooled_planes", u - 2][:, 0, :],
                     rhs=w1_codes[:, 0, : bank.shape[2]].bitcast(FP8X4),
-                    rhs_scale=w1_planes[:, 0, : bank.shape[2]],
+                    rhs_scale=w1_plane(0, slice(0, bank.shape[2])),
                     start=True,
                     stop=True,
                 )
@@ -203,7 +229,7 @@ def tile_semanticaligner_e_kernel(
                     lhsT=tiles["pooled_codes", u][:, g, :].bitcast(FP8X4),
                     lhsT_scale=tiles["pooled_planes", u][:, g, :],
                     rhs=w1_codes[:, m * PASSES + g, cols].bitcast(FP8X4),
-                    rhs_scale=w1_planes[:, m * PASSES + g, cols],
+                    rhs_scale=w1_plane(m * PASSES + g, cols),
                     start=(g == 0),
                     stop=(g == PASSES - 1),
                 )

@@ -33,6 +33,8 @@ QUADRANT = 32
 SCALE_ROWS = 4
 PLANES = 4
 
+AHEAD = 2
+
 FLOPS = 2 * MODS * B * D * (D + PROJ)
 
 
@@ -82,6 +84,10 @@ def tile_semanticaligner_e_kernel(
 
         neg_half = const.tile([P, 1], F32)
         nc.vector.memset(neg_half[:], -0.5)
+        eps_col = const.tile([P, 1], F32)
+        nc.vector.tensor_scalar(
+            out=eps_col[:], in0=neg_half[:], scalar1=-2.0 * LN_EPS, scalar2=None, op0=ALU.mult
+        )
         warm = const.tile([P, 1], F32)
         nc.scalar.activation(out=warm[:], in_=neg_half[:], func=ACT.Gelu)
 
@@ -100,6 +106,7 @@ def tile_semanticaligner_e_kernel(
         w1_codes = weights.tile([P, MODS * PASSES, D], U32, align_bytes=64)
         w2_codes = weights.tile([P, MODS * PASSES, PROJ], U32, align_bytes=64)
         chunks = {}
+
         def load_w1_scales(first, quadrant):
             passes = min(PLANES, MODS * PASSES - first)
             rows = slice(quadrant * SCALE_ROWS, (quadrant + 1) * SCALE_ROWS)
@@ -172,6 +179,27 @@ def tile_semanticaligner_e_kernel(
 
         tiles = {}
 
+        def is_split(u, q):
+            return False
+
+        def split(u, q):
+            if is_split(u, q):
+                apart = work.tile([P, GROUPS * PASSES, 2, P, 2], BF16, tag="apart")
+                nc.vector.tensor_copy(
+                    out=apart[:].rearrange("p x s w e -> p (x s w e)").bitcast(I32).rearrange(
+                        "p (x s w) -> p x s w", x=GROUPS * PASSES, s=2
+                    ),
+                    in_=chunks[u, q][:].rearrange("p j d -> p (j d)").bitcast(I32).rearrange(
+                        "p (x w s) -> p x s w", x=GROUPS * PASSES, s=2
+                    ),
+                )
+                tiles["apart", u, q] = apart
+
+        def stationary(u, q, j, g, t):
+            if is_split(u, q):
+                return tiles["apart", u, q][:, j * PASSES + g, t // 2, :, t % 2]
+            return chunks[u, q][:, j, g * K_PASS + t : (g + 1) * K_PASS : PACK]
+
         def pool(u, q):
             if q == 0:
                 tiles["pooled", u] = work.tile(
@@ -195,7 +223,7 @@ def tile_semanticaligner_e_kernel(
                     for t in range(PACK):
                         nc.tensor.matmul(
                             out=mean_ps[:, g, t, rows],
-                            lhsT=chunks[u, q][:, j, g * K_PASS + t : (g + 1) * K_PASS : PACK],
+                            lhsT=stationary(u, q, j, g, t),
                             rhs=selector[:],
                             start=True,
                             stop=True,
@@ -299,34 +327,60 @@ def tile_semanticaligner_e_kernel(
                 )
             tiles["z_ps", u] = z_ps
 
+        def add_b2(u):
+            m = u // HALVES
+            z = work.tile([P, PROJ], F32, tag="z")
+            stats = small.tile([P, PROJ_TILES, 6], F32, tag="stats")
+            for i in range(PROJ_TILES):
+                cols = slice(i * P, (i + 1) * P)
+                nc.vector.tensor_tensor(
+                    out=z[:, cols],
+                    in0=tiles["z_ps", u][:, cols],
+                    in1=everywhere["b2"][:, m * PROJ + i * P : m * PROJ + (i + 1) * P],
+                    op=ALU.add,
+                )
+            for i in range(PROJ_TILES):
+                nc.vector.bn_stats(out=stats[:, i, :], in_=z[:, i * P : (i + 1) * P])
+            mean_var = small.tile([P, 2], F32, tag="mean_var")
+            nc.vector.bn_aggr(out=mean_var[:], in_=stats[:].rearrange("p i s -> p (i s)"))
+            tiles["z", u] = z
+            tiles["mean_var", u] = mean_var
+
         def centre(u):
             m = u // HALVES
-            of_m = slice(m * PROJ, (m + 1) * PROJ)
-            z = work.tile([P, PROJ], F32, tag="z")
-            nc.vector.tensor_tensor(
-                out=z[:], in0=tiles["z_ps", u][:], in1=everywhere["b2"][:, of_m], op=ALU.add
-            )
-            stats = small.tile([P, 6], F32, tag="stats")
-            nc.vector.bn_stats(out=stats[:], in_=z[:])
-            mean_var = small.tile([P, 2], F32, tag="mean_var")
-            nc.vector.bn_aggr(out=mean_var[:], in_=stats[:])
-            var_eps = small.tile([P, 1], F32, tag="var_eps")
-            nc.gpsimd.tensor_scalar(
-                out=var_eps[:], in0=mean_var[:, 1:2], scalar1=LN_EPS, scalar2=None, op0=ALU.add
-            )
-            rstd = small.tile([P, 1], F32, tag="rstd")
-            nc.gpsimd.tensor_tensor(out=rstd[:], in0=var_eps[:], in1=neg_half[:], op=ALU.pow)
             centred = work.tile([P, PROJ], F32, tag="centred")
             nc.vector.scalar_tensor_tensor(
                 out=centred[:],
-                in0=z[:],
-                scalar=mean_var[:, 0:1],
-                in1=everywhere["gamma"][:, of_m],
+                in0=tiles["z", u][:],
+                scalar=tiles["mean_var", u][:, 0:1],
+                in1=everywhere["gamma"][:, m * PROJ : (m + 1) * PROJ],
                 op0=ALU.subtract,
                 op1=ALU.mult,
             )
             tiles["centred", u] = centred
-            tiles["rstd", u] = rstd
+
+        def inverse_root(name, u, column):
+            root = small.tile([P, 1], F32, tag=name, name=name)
+            nc.gpsimd.tensor_tensor(out=root[:], in0=column, in1=neg_half[:], op=ALU.pow)
+            tiles[name, u] = root
+
+        def inverse_root_scalar(name, u, column, bias):
+            root = small.tile([P, 1], F32, tag=name, name=name)
+            nc.scalar.activation(
+                out=root[:], in_=column, func=ACT.Abs_reciprocal_sqrt, bias=bias
+            )
+            tiles[name, u] = root
+
+        def inverse_deviation(u):
+            var_eps = small.tile([P, 1], F32, tag="var_eps")
+            nc.gpsimd.tensor_scalar(
+                out=var_eps[:],
+                in0=tiles["mean_var", u][:, 1:2],
+                scalar1=LN_EPS,
+                scalar2=None,
+                op0=ALU.add,
+            )
+            inverse_root("rstd", u, var_eps[:])
 
         def normalise(u):
             m = u // HALVES
@@ -341,19 +395,29 @@ def tile_semanticaligner_e_kernel(
             )
             tiles["y", u] = y
 
-        def inverse_norm(u):
+        def sum_squares(u):
             squares = work.tile([P, PROJ], F32, tag="squares")
             sum_sq = small.tile([P, 1], F32, tag="sum_sq")
             nc.scalar.activation(
                 out=squares[:], in_=tiles["y", u][:], func=ACT.Square, accum_out=sum_sq[:]
             )
+            tiles["sum_sq", u] = sum_sq
+
+        def floor_norm(engine, u):
             floored = small.tile([P, 1], F32, tag="floored")
-            nc.gpsimd.tensor_scalar(
-                out=floored[:], in0=sum_sq[:], scalar1=NORM_EPS * NORM_EPS, scalar2=None, op0=ALU.max
+            engine.tensor_scalar(
+                out=floored[:],
+                in0=tiles["sum_sq", u][:],
+                scalar1=NORM_EPS * NORM_EPS,
+                scalar2=None,
+                op0=ALU.max,
             )
-            rnorm = small.tile([P, 1], F32, tag="rnorm")
-            nc.gpsimd.tensor_tensor(out=rnorm[:], in0=floored[:], in1=neg_half[:], op=ALU.pow)
-            tiles["rnorm", u] = rnorm
+            tiles["floored", u] = floored
+
+        def inverse_norm(u):
+            sum_squares(u)
+            floor_norm(nc.gpsimd, u)
+            inverse_root("rnorm", u, tiles["floored", u][:])
 
         def finish(u):
             result = results.tile([P, PROJ], F32, tag="result")
@@ -375,62 +439,75 @@ def tile_semanticaligner_e_kernel(
                 for n in range(PASSES):
                     work_of(u, n)
 
+        split_order = [(u, q) for u in range(UNITS) for q in range(CHUNKS)]
+
+        def take_in(u, q):
+            ahead = split_order.index((u, q)) + AHEAD
+            if ahead < len(split_order):
+                split(*split_order[ahead])
+            pool(u, q)
+            round_mean(u, q)
+
         for u in range(UNITS):
             m, half = divmod(u, HALVES)
-            pool(u, 0)
-            round_mean(u, 0)
-            both(turn_h, u - 2)
-            stage(normalise, u - 3)
-            stage(inverse_norm, u - 3)
-            both(group_h, u - 2)
-            both(quantise_h, u - 2)
-            pool(u, 1)
-            round_mean(u, 1)
+            take_in(u, 0)
             stage(finish, u - 3)
+            both(first_matmul, u - 1)
+            stage(second_matmul, u - 2)
+            both(add_bias, u - 1)
+            both(gelu, u - 1)
+            stage(add_b2, u - 2)
+            stage(inverse_deviation, u - 2)
+            stage(centre, u - 2)
+            take_in(u, 1)
             if u == 0:
                 turn_vectors()
-            both(first_matmul, u - 1)
-            both(add_bias, u - 1)
-            stage(gelu, u - 1, 0)
-            pool(u, 2)
-            round_mean(u, 2)
-            stage(gelu, u - 1, 1)
-            if half == 0:
-                spread("b1_%d" % m, first_row["b1"] + m * F_TILES, F_TILES)
-            stage(second_matmul, u - 2)
-            stage(centre, u - 2)
-            pool(u, 3)
-            round_mean(u, 3)
+                spread("b1_0", first_row["b1"], F_TILES)
+            take_in(u, 2)
+            both(turn_h, u - 1)
+            both(group_h, u - 1)
+            stage(normalise, u - 2)
+            both(quantise_h, u - 1)
             if u == 0:
-                for name in ("b2", "gamma", "beta"):
+                for name in ("b2", "gamma"):
                     spread(name, first_row[name], MODS * PROJ_TILES)
+            take_in(u, 3)
+            if u == 0:
+                spread("beta", first_row["beta"], MODS * PROJ_TILES)
+            if half == 1 and m + 1 < MODS:
+                spread("b1_%d" % (m + 1), first_row["b1"] + (m + 1) * F_TILES, F_TILES)
+            stage(inverse_norm, u - 2)
             quantise_pooled(u)
 
         last = UNITS - 1
-        both(turn_h, last - 1)
-        both(group_h, last - 1)
-        both(quantise_h, last - 1)
-        normalise(last - 2)
         for u in range(last - 2):
             store(nc.scalar, u)
         both(first_matmul, last)
+        second_matmul(last - 1)
         both(add_bias, last)
         both(gelu, last)
-        inverse_norm(last - 2)
-        second_matmul(last - 1)
+        finish(last - 2)
+        store(nc.sync, last - 2)
+        add_b2(last - 1)
+        inverse_deviation(last - 1)
         centre(last - 1)
         both(turn_h, last)
         both(group_h, last)
         both(quantise_h, last)
-        finish(last - 2)
-        store(nc.sync, last - 2)
+        nc.scalar.activation(out=warm[:], in_=eps_col[:], func=ACT.Abs_reciprocal_sqrt)
         normalise(last - 1)
         second_matmul(last)
+        sum_squares(last - 1)
+        add_b2(last)
+        inverse_root_scalar("rstd", last, tiles["mean_var", last][:, 1:2], eps_col[:])
         centre(last)
-        inverse_norm(last - 1)
         normalise(last)
-        inverse_norm(last)
+        floor_norm(nc.gpsimd, last - 1)
+        inverse_root_scalar("rnorm", last - 1, tiles["floored", last - 1][:], 0.0)
         finish(last - 1)
         store(nc.sync, last - 1)
+        sum_squares(last)
+        floor_norm(nc.vector, last)
+        inverse_root_scalar("rnorm", last, tiles["floored", last][:], 0.0)
         finish(last)
         store(nc.sync, last)

@@ -33,8 +33,6 @@ QUADRANT = 32
 SCALE_ROWS = 4
 PLANES = 4
 
-AHEAD = 2
-
 FLOPS = 2 * MODS * B * D * (D + PROJ)
 
 
@@ -47,7 +45,7 @@ def tile_semanticaligner_e_kernel(
         weights = ctx.enter_context(tc.tile_pool(name="weights", bufs=1))
         loads = ctx.enter_context(tc.tile_pool(name="loads", bufs=UNITS * CHUNKS))
         work = ctx.enter_context(tc.tile_pool(name="work", bufs=3))
-        results = ctx.enter_context(tc.tile_pool(name="results", bufs=UNITS))
+        kept = ctx.enter_context(tc.tile_pool(name="kept", bufs=UNITS))
         small = ctx.enter_context(tc.tile_pool(name="small", bufs=3))
         pool_psum = ctx.enter_context(tc.psum_pool(name="pool_psum", bufs=3))
         turn_psum = ctx.enter_context(tc.psum_pool(name="turn_psum", bufs=2))
@@ -87,6 +85,22 @@ def tile_semanticaligner_e_kernel(
         eps_col = const.tile([P, 1], F32)
         nc.vector.tensor_scalar(
             out=eps_col[:], in0=neg_half[:], scalar1=-2.0 * LN_EPS, scalar2=None, op0=ALU.mult
+        )
+        eps2_col = const.tile([P, 1], F32)
+        nc.vector.tensor_scalar(
+            out=eps2_col[:],
+            in0=neg_half[:],
+            scalar1=-2.0 * NORM_EPS * NORM_EPS,
+            scalar2=None,
+            op0=ALU.mult,
+        )
+        minus_eps2_col = const.tile([P, 1], F32)
+        nc.vector.tensor_scalar(
+            out=minus_eps2_col[:],
+            in0=neg_half[:],
+            scalar1=2.0 * NORM_EPS * NORM_EPS,
+            scalar2=None,
+            op0=ALU.mult,
         )
         warm = const.tile([P, 1], F32)
         nc.scalar.activation(out=warm[:], in_=neg_half[:], func=ACT.Gelu)
@@ -147,16 +161,18 @@ def tile_semanticaligner_e_kernel(
                 load(*args)
             scale_loads[:count] = []
 
-        for m in range(MODS):
+        pieces = {}
+        for m, first in enumerate((3, 11, 19)):
             of_m = m * PASSES
-            pieces = [(w1_codes, w1_words, of_m + g, of_m + g + 1) for g in range(PASSES)]
-            pieces.append((w2_codes, w2_words, of_m, of_m + PASSES))
-            for i in range(HALVES * CHUNKS):
-                load_chunk(m * HALVES + i // CHUNKS, i % CHUNKS)
-                if i >= 2:
-                    load_some_scales(2)
-                if CHUNKS - 1 <= i < CHUNKS - 1 + len(pieces):
-                    load_weights(*pieces[i - CHUNKS + 1])
+            for g in range(PASSES):
+                pieces[first + g] = (w1_codes, w1_words, of_m + g, of_m + g + 1)
+            pieces[first + PASSES] = (w2_codes, w2_words, of_m, of_m + PASSES)
+        for i in range(UNITS * CHUNKS):
+            load_chunk(i // CHUNKS, i % CHUNKS)
+            if i >= 2:
+                load_some_scales(2)
+            if i in pieces:
+                load_weights(*pieces[i])
 
         everywhere = {}
         vector_cols = const.tile([P, P], BF16)
@@ -178,27 +194,6 @@ def tile_semanticaligner_e_kernel(
             nc.scalar.copy(out=everywhere[name][:], in_=bank[:])
 
         tiles = {}
-
-        def is_split(u, q):
-            return False
-
-        def split(u, q):
-            if is_split(u, q):
-                apart = work.tile([P, GROUPS * PASSES, 2, P, 2], BF16, tag="apart")
-                nc.vector.tensor_copy(
-                    out=apart[:].rearrange("p x s w e -> p (x s w e)").bitcast(I32).rearrange(
-                        "p (x s w) -> p x s w", x=GROUPS * PASSES, s=2
-                    ),
-                    in_=chunks[u, q][:].rearrange("p j d -> p (j d)").bitcast(I32).rearrange(
-                        "p (x w s) -> p x s w", x=GROUPS * PASSES, s=2
-                    ),
-                )
-                tiles["apart", u, q] = apart
-
-        def stationary(u, q, j, g, t):
-            if is_split(u, q):
-                return tiles["apart", u, q][:, j * PASSES + g, t // 2, :, t % 2]
-            return chunks[u, q][:, j, g * K_PASS + t : (g + 1) * K_PASS : PACK]
 
         def pool(u, q):
             if q == 0:
@@ -223,7 +218,7 @@ def tile_semanticaligner_e_kernel(
                     for t in range(PACK):
                         nc.tensor.matmul(
                             out=mean_ps[:, g, t, rows],
-                            lhsT=stationary(u, q, j, g, t),
+                            lhsT=chunks[u, q][:, j, g * K_PASS + t : (g + 1) * K_PASS : PACK],
                             rhs=selector[:],
                             start=True,
                             stop=True,
@@ -237,8 +232,8 @@ def tile_semanticaligner_e_kernel(
             )
 
         def quantise_pooled(u):
-            codes = work.tile([P, PASSES, P], U32, tag="pooled_codes", align_bytes=64)
-            planes = work.tile([P, PASSES, P], U8, tag="pooled_planes", align_bytes=64)
+            codes = kept.tile([P, PASSES, P], U32, tag="pooled_codes", align_bytes=64)
+            planes = kept.tile([P, PASSES, P], U8, tag="pooled_planes", align_bytes=64)
             nc.vector.quantize_mx(
                 out=codes[:].rearrange("p g r -> p (g r)").bitcast(FP8X4),
                 scales=planes[:].rearrange("p g r -> p (g r)"),
@@ -373,7 +368,7 @@ def tile_semanticaligner_e_kernel(
 
         def inverse_deviation(u):
             var_eps = small.tile([P, 1], F32, tag="var_eps")
-            nc.gpsimd.tensor_scalar(
+            nc.vector.tensor_scalar(
                 out=var_eps[:],
                 in0=tiles["mean_var", u][:, 1:2],
                 scalar1=LN_EPS,
@@ -403,26 +398,39 @@ def tile_semanticaligner_e_kernel(
             )
             tiles["sum_sq", u] = sum_sq
 
-        def floor_norm(engine, u):
+        def inverse_norm(u):
             floored = small.tile([P, 1], F32, tag="floored")
-            engine.tensor_scalar(
+            nc.vector.tensor_scalar(
                 out=floored[:],
                 in0=tiles["sum_sq", u][:],
                 scalar1=NORM_EPS * NORM_EPS,
                 scalar2=None,
                 op0=ALU.max,
             )
-            tiles["floored", u] = floored
+            inverse_root("rnorm", u, floored[:])
 
-        def inverse_norm(u):
-            sum_squares(u)
-            floor_norm(nc.gpsimd, u)
-            inverse_root("rnorm", u, tiles["floored", u][:])
+        def inverse_norm_scalar(u):
+            excess = small.tile([P, 1], F32, tag="excess")
+            nc.scalar.activation(
+                out=excess[:], in_=tiles["sum_sq", u][:], func=ACT.Relu, bias=minus_eps2_col[:]
+            )
+            inverse_root_scalar("rnorm", u, excess[:], eps2_col[:])
 
         def finish(u):
-            result = results.tile([P, PROJ], F32, tag="result")
+            result = kept.tile([P, PROJ], F32, tag="result")
             nc.scalar.activation(
                 out=result[:], in_=tiles["y", u][:], func=ACT.Copy, scale=tiles["rnorm", u][:]
+            )
+            tiles["result", u] = result
+
+        def finish_on_vector(u):
+            result = kept.tile([P, PROJ], F32, tag="result")
+            nc.vector.tensor_scalar(
+                out=result[:],
+                in0=tiles["y", u][:],
+                scalar1=tiles["rnorm", u][:],
+                scalar2=None,
+                op0=ALU.mult,
             )
             tiles["result", u] = result
 
@@ -439,55 +447,52 @@ def tile_semanticaligner_e_kernel(
                 for n in range(PASSES):
                     work_of(u, n)
 
-        split_order = [(u, q) for u in range(UNITS) for q in range(CHUNKS)]
-
         def take_in(u, q):
-            ahead = split_order.index((u, q)) + AHEAD
-            if ahead < len(split_order):
-                split(*split_order[ahead])
             pool(u, q)
             round_mean(u, q)
 
         for u in range(UNITS):
             m, half = divmod(u, HALVES)
             take_in(u, 0)
-            stage(finish, u - 3)
+            stage(inverse_norm, u - 3)
             both(first_matmul, u - 1)
             stage(second_matmul, u - 2)
             both(add_bias, u - 1)
             both(gelu, u - 1)
+            stage(finish_on_vector, u - 3)
             stage(add_b2, u - 2)
-            stage(inverse_deviation, u - 2)
             stage(centre, u - 2)
+            stage(inverse_deviation, u - 2)
             take_in(u, 1)
-            if u == 0:
-                turn_vectors()
-                spread("b1_0", first_row["b1"], F_TILES)
+            if u == 1:
+                spread("beta", first_row["beta"], MODS * PROJ_TILES)
             take_in(u, 2)
             both(turn_h, u - 1)
             both(group_h, u - 1)
-            stage(normalise, u - 2)
             both(quantise_h, u - 1)
+            stage(normalise, u - 2)
             if u == 0:
-                for name in ("b2", "gamma"):
-                    spread(name, first_row[name], MODS * PROJ_TILES)
+                turn_vectors()
             take_in(u, 3)
             if u == 0:
-                spread("beta", first_row["beta"], MODS * PROJ_TILES)
+                spread("b1_0", first_row["b1"], F_TILES)
+                for name in ("b2", "gamma"):
+                    spread(name, first_row[name], MODS * PROJ_TILES)
             if half == 1 and m + 1 < MODS:
                 spread("b1_%d" % (m + 1), first_row["b1"] + (m + 1) * F_TILES, F_TILES)
-            stage(inverse_norm, u - 2)
+            stage(sum_squares, u - 2)
             quantise_pooled(u)
 
         last = UNITS - 1
-        for u in range(last - 2):
-            store(nc.scalar, u)
         both(first_matmul, last)
         second_matmul(last - 1)
+        inverse_norm(last - 2)
         both(add_bias, last)
         both(gelu, last)
-        finish(last - 2)
+        finish_on_vector(last - 2)
         store(nc.sync, last - 2)
+        for u in range(last - 2):
+            store(nc.sync, u)
         add_b2(last - 1)
         inverse_deviation(last - 1)
         centre(last - 1)
@@ -501,13 +506,11 @@ def tile_semanticaligner_e_kernel(
         add_b2(last)
         inverse_root_scalar("rstd", last, tiles["mean_var", last][:, 1:2], eps_col[:])
         centre(last)
+        inverse_norm_scalar(last - 1)
         normalise(last)
-        floor_norm(nc.gpsimd, last - 1)
-        inverse_root_scalar("rnorm", last - 1, tiles["floored", last - 1][:], 0.0)
-        finish(last - 1)
+        finish_on_vector(last - 1)
         store(nc.sync, last - 1)
         sum_squares(last)
-        floor_norm(nc.vector, last)
-        inverse_root_scalar("rnorm", last, tiles["floored", last][:], 0.0)
+        inverse_norm_scalar(last)
         finish(last)
         store(nc.sync, last)

from contextlib import ExitStack

import concourse.mybir as mybir
from concourse.masks import make_identity

BF16 = mybir.dt.bfloat16
F32 = mybir.dt.float32
I32 = mybir.dt.int32
U32 = mybir.dt.uint32
U8 = mybir.dt.uint8
FP8X4 = mybir.dt.float8_e4m3fn_x4
ACT = mybir.ActivationFunctionType
ALU = mybir.AluOpType
AXIS = mybir.AxisListType

P = 128
MODS, B, T, D, PROJ = 3, 256, 8, 1024, 256
LN_EPS = 1e-5
NORM_EPS = 1e-12

PACK = 4
K_PASS = P * PACK
PASSES = D // K_PASS
F_TILES = D // P
PROJ_TILES = PROJ // P
HALVES = B // P
UNITS = MODS * HALVES
GROUP_B = P // T
CHUNK_B = 32
GROUPS = CHUNK_B // GROUP_B
CHUNKS = P // CHUNK_B
QUADRANT = 32
SCALE_ROWS = 4
PLANES = 4

FLOPS = 2 * MODS * B * D * (D + PROJ)


def tile_semanticaligner_e_kernel(
    tc, feats, w1_words, w1_scales, b1, w2_words, w2_scales, b2, gamma, beta, out
):
    nc = tc.nc
    with ExitStack() as ctx:
        const = ctx.enter_context(tc.tile_pool(name="const", bufs=1))
        weights = ctx.enter_context(tc.tile_pool(name="weights", bufs=1))
        loads = ctx.enter_context(tc.tile_pool(name="loads", bufs=UNITS * CHUNKS))
        work = ctx.enter_context(tc.tile_pool(name="work", bufs=3))
        kept = ctx.enter_context(tc.tile_pool(name="kept", bufs=UNITS))
        small = ctx.enter_context(tc.tile_pool(name="small", bufs=3))
        pool_psum = ctx.enter_context(tc.psum_pool(name="pool_psum", bufs=3))
        turn_psum = ctx.enter_context(tc.psum_pool(name="turn_psum", bufs=2))
        mx_psum = ctx.enter_context(tc.psum_pool(name="mx_psum", bufs=3))
        ctx.enter_context(tc.manual_schedule())

        w1_planes = []
        for first in range(0, MODS * PASSES, PLANES):
            shared = weights.tile([P, D], U8, name="w1_planes%d" % first, align_bytes=64)
            nc.vector.memset(shared[:].bitcast(I32), 0)
            w1_planes.append(shared)
        w2_planes = weights.tile([P, MODS * PASSES, PROJ], U8, align_bytes=64)
        nc.vector.memset(w2_planes[:].bitcast(I32), 0)

        def w1_plane(i, cols):
            return w1_planes[i // PLANES][i % PLANES * SCALE_ROWS :, cols]

        vector_rows = const.tile([P, P], BF16)
        nc.vector.memset(vector_rows[:], 0.0)
        first_row = {}
        next_row = 0
        for name, vector in (("b1", b1), ("b2", b2), ("gamma", gamma), ("beta", beta)):
            as_rows = vector.rearrange("m (c f) -> (m c) f", f=P)
            first_row[name] = next_row
            nc.scalar.dma_start(
                out=vector_rows[next_row : next_row + as_rows.shape[0], :], in_=as_rows
            )
            next_row += as_rows.shape[0]

        ident_bf = const.tile([P, P], BF16)
        make_identity(nc, ident_bf[:])
        ident_f32 = const.tile([P, P], F32)
        make_identity(nc, ident_f32[:])

        neg_half = const.tile([P, 1], F32)
        nc.vector.memset(neg_half[:], -0.5)
        eps_col = const.tile([P, 1], F32)
        nc.vector.tensor_scalar(
            out=eps_col[:], in0=neg_half[:], scalar1=-2.0 * LN_EPS, scalar2=None, op0=ALU.mult
        )
        eps2_col = const.tile([P, 1], F32)
        nc.vector.tensor_scalar(
            out=eps2_col[:],
            in0=neg_half[:],
            scalar1=-2.0 * NORM_EPS * NORM_EPS,
            scalar2=None,
            op0=ALU.mult,
        )
        minus_eps2_col = const.tile([P, 1], F32)
        nc.vector.tensor_scalar(
            out=minus_eps2_col[:],
            in0=neg_half[:],
            scalar1=2.0 * NORM_EPS * NORM_EPS,
            scalar2=None,
            op0=ALU.mult,
        )
        warm = const.tile([P, 1], F32)
        nc.scalar.activation(out=warm[:], in_=neg_half[:], func=ACT.Gelu)

        selector_f32 = const.tile([P, GROUP_B], F32)
        nc.vector.tensor_reduce(
            out=selector_f32[:],
            in_=ident_bf[:].rearrange("p (r t) -> p r t", t=T),
            axis=AXIS.X,
            op=ALU.add,
        )
        selector = const.tile([P, GROUP_B], BF16)
        nc.vector.tensor_scalar(
            out=selector[:], in0=selector_f32[:], scalar1=1.0 / T, scalar2=None, op0=ALU.mult
        )

        w1_codes = weights.tile([P, MODS * PASSES, D], U32, align_bytes=64)
        w2_codes = weights.tile([P, MODS * PASSES, PROJ], U32, align_bytes=64)
        chunks = {}

        def load_w1_scales(first, quadrant):
            passes = min(PLANES, MODS * PASSES - first)
            rows = slice(quadrant * SCALE_ROWS, (quadrant + 1) * SCALE_ROWS)
            start = quadrant * QUADRANT
            nc.sync.dma_start(
                out=w1_planes[first // PLANES][start : start + passes * SCALE_ROWS, :].bitcast(I32),
                in_=w1_scales[first : first + passes, rows, :].bitcast(I32),
            )

        def load_w2_scales(r):
            nc.sync.dma_start(
                out=w2_planes[r:P:QUADRANT, :, :].bitcast(I32),
                in_=w2_scales.rearrange("g (q r) n -> r q g n", r=SCALE_ROWS)[r].bitcast(I32),
            )

        def load_weights(codes, words, first, end):
            nc.sync.dma_start(
                out=codes[:, first:end, :].bitcast(I32),
                in_=words[first:end].rearrange("g p n t -> p g (n t)").bitcast(I32),
            )

        def load_chunk(u, c):
            m, half = divmod(u, HALVES)
            first = half * P + c * CHUNK_B
            chunk = loads.tile([P, GROUPS, D], BF16, tag="chunk")
            nc.sync.dma_start(
                out=chunk[:],
                in_=feats[m, first : first + CHUNK_B].rearrange("(j r) t d -> (r t) j d", r=GROUP_B),
            )
            chunks[u, c] = chunk

        scale_loads = [(load_w1_scales, 0, q) for q in range(P // QUADRANT)]
        scale_loads += [(load_w2_scales, r) for r in range(SCALE_ROWS)]
        scale_loads += [(load_w1_scales, PLANES, q) for q in range(P // QUADRANT)]

        def load_some_scales(count):
            for load, *args in scale_loads[:count]:
                load(*args)
            scale_loads[:count] = []

        pieces = {}
        for m, first in enumerate((3, 11, 19)):
            of_m = m * PASSES
            for g in range(PASSES):
                pieces[first + g] = (w1_codes, w1_words, of_m + g, of_m + g + 1)
            pieces[first + PASSES] = (w2_codes, w2_words, of_m, of_m + PASSES)
        for i in range(UNITS * CHUNKS):
            load_chunk(i // CHUNKS, i % CHUNKS)
            if i >= 2:
                load_some_scales(2)
            if i in pieces:
                load_weights(*pieces[i])

        everywhere = {}
        vector_cols = const.tile([P, P], BF16)

        def turn_vectors():
            cols_ps = turn_psum.tile([P, P], BF16, tag="turn")
            nc.tensor.transpose(cols_ps[:], vector_rows[:], ident_bf[:])
            nc.vector.tensor_copy(out=vector_cols[:], in_=cols_ps[:])

        def spread(name, first, count):
            bank = turn_psum.tile([P, count * P], BF16, tag="turn")
            for i in range(count):
                nc.tensor.transpose(
                    bank[:, i * P : (i + 1) * P],
                    vector_cols[:, first + i : first + i + 1].to_broadcast([P, P]),
                    ident_bf[:],
                )
            everywhere[name] = const.tile([P, count * P], BF16, name=name)
            nc.scalar.copy(out=everywhere[name][:], in_=bank[:])

        tiles = {}

        def pool(u, q):
            if q == 0:
                tiles["pooled", u] = work.tile(
                    [P, PASSES, P, PACK], BF16, tag="pooled", name="pooled", align_bytes=64
                )
            bank = pool_psum.tile([P, 2, PASSES * PACK * CHUNK_B], F32, tag="mean")
            if u >= 2:
                nc.tensor.matmul_mx(
                    out=bank[:, 1, :],
                    lhsT=tiles["pooled_codes", u - 2][:, 0, :].bitcast(FP8X4),
                    lhsT_scale=tiles["pooled_planes", u - 2][:, 0, :],
                    rhs=w1_codes[:, 0, : bank.shape[2]].bitcast(FP8X4),
                    rhs_scale=w1_plane(0, slice(0, bank.shape[2])),
                    start=True,
                    stop=True,
                )
            mean_ps = bank[:, 0, :].rearrange("p (g t r) -> p g t r", g=PASSES, t=PACK)
            for j in range(GROUPS):
                rows = slice(j * GROUP_B, (j + 1) * GROUP_B)
                for g in range(PASSES):
                    for t in range(PACK):
                        nc.tensor.matmul(
                            out=mean_ps[:, g, t, rows],
                            lhsT=chunks[u, q][:, j, g * K_PASS + t : (g + 1) * K_PASS : PACK],
                            rhs=selector[:],
                            start=True,
                            stop=True,
                        )
            tiles["mean_ps", u, q] = mean_ps

        def round_mean(u, q):
            nc.scalar.copy(
                out=tiles["pooled", u][:, :, q * CHUNK_B : (q + 1) * CHUNK_B, :],
                in_=tiles["mean_ps", u, q].rearrange("p g t r -> p g r t"),
            )

        def quantise_pooled(u):
            codes = kept.tile([P, PASSES, P], U32, tag="pooled_codes", align_bytes=64)
            planes = kept.tile([P, PASSES, P], U8, tag="pooled_planes", align_bytes=64)
            nc.vector.quantize_mx(
                out=codes[:].rearrange("p g r -> p (g r)").bitcast(FP8X4),
                scales=planes[:].rearrange("p g r -> p (g r)"),
                in_=tiles["pooled", u][:].rearrange("p g r t -> p (g r t)"),
            )
            tiles["pooled_codes", u] = codes
            tiles["pooled_planes", u] = planes

        def first_matmul(u, n):
            m = u // HALVES
            cols = slice(n * K_PASS, (n + 1) * K_PASS)
            acc = mx_psum.tile([P, K_PASS], F32, tag="acc")
            for g in range(PASSES):
                nc.tensor.matmul_mx(
                    out=acc[:],
                    lhsT=tiles["pooled_codes", u][:, g, :].bitcast(FP8X4),
                    lhsT_scale=tiles["pooled_planes", u][:, g, :],
                    rhs=w1_codes[:, m * PASSES + g, cols].bitcast(FP8X4),
                    rhs_scale=w1_plane(m * PASSES + g, cols),
                    start=(g == 0),
                    stop=(g == PASSES - 1),
                )
            tiles["acc", u, n] = acc

        def add_bias(u, n):
            cols = slice(n * K_PASS, (n + 1) * K_PASS)
            pre = work.tile([P, K_PASS], F32, tag="pre")
            nc.vector.tensor_tensor(
                out=pre[:],
                in0=tiles["acc", u, n][:],
                in1=everywhere["b1_%d" % (u // HALVES)][:, cols],
                op=ALU.add,
            )
            tiles["pre", u, n] = pre

        def gelu(u, n):
            h_words = work.tile([P, 2, P, 2], BF16, tag="h_words")
            nc.scalar.activation(
                out=h_words[:],
                in_=tiles["pre", u, n][:].rearrange("r (p s e) -> r s p e", s=2, e=2),
                func=ACT.Gelu,
            )
            tiles["h_words", u, n] = h_words

        def turn_h(u, n):
            word_ps = turn_psum.tile([P, 2, P], F32, tag="turn")
            for s in range(2):
                nc.tensor.transpose(
                    word_ps[:, s, :],
                    tiles["h_words", u, n][:, s].rearrange("r p e -> r (p e)").bitcast(F32),
                    ident_f32[:],
                )
            tiles["word_ps", u, n] = word_ps

        def group_h(u, n):
            grouped = work.tile([P, P, PACK], BF16, tag="h_grouped", align_bytes=64)
            nc.scalar.copy(
                out=grouped[:].bitcast(F32),
                in_=tiles["word_ps", u, n][:].rearrange("p s r -> p r s"),
            )
            tiles["grouped", u, n] = grouped

        def quantise_h(u, n):
            codes = work.tile([P, P], U32, tag="h_codes%d" % n, name="h_codes", align_bytes=64)
            planes = work.tile([P, P], U8, tag="h_planes%d" % n, name="h_planes", align_bytes=64)
            nc.vector.quantize_mx(
                out=codes[:].bitcast(FP8X4),
                scales=planes[:],
                in_=tiles["grouped", u, n][:].rearrange("p r t -> p (r t)"),
            )
            tiles["h_codes", u, n] = codes
            tiles["h_planes", u, n] = planes

        def second_matmul(u):
            m = u // HALVES
            z_ps = mx_psum.tile([P, PROJ], F32, tag="acc")
            for g in range(PASSES):
                nc.tensor.matmul_mx(
                    out=z_ps[:],
                    lhsT=tiles["h_codes", u, g][:].bitcast(FP8X4),
                    lhsT_scale=tiles["h_planes", u, g][:],
                    rhs=w2_codes[:, m * PASSES + g, :].bitcast(FP8X4),
                    rhs_scale=w2_planes[:, m * PASSES + g, :],
                    start=(g == 0),
                    stop=(g == PASSES - 1),
                )
            tiles["z_ps", u] = z_ps

        def add_b2(u):
            m = u // HALVES
            z = work.tile([P, PROJ], F32, tag="z")
            stats = small.tile([P, PROJ_TILES, 6], F32, tag="stats")
            for i in range(PROJ_TILES):
                cols = slice(i * P, (i + 1) * P)
                nc.vector.tensor_tensor(
                    out=z[:, cols],
                    in0=tiles["z_ps", u][:, cols],
                    in1=everywhere["b2"][:, m * PROJ + i * P : m * PROJ + (i + 1) * P],
                    op=ALU.add,
                )
            for i in range(PROJ_TILES):
                nc.vector.bn_stats(out=stats[:, i, :], in_=z[:, i * P : (i + 1) * P])
            mean_var = small.tile([P, 2], F32, tag="mean_var")
            nc.vector.bn_aggr(out=mean_var[:], in_=stats[:].rearrange("p i s -> p (i s)"))
            tiles["z", u] = z
            tiles["mean_var", u] = mean_var

        def centre(u):
            m = u // HALVES
            centred = work.tile([P, PROJ], F32, tag="centred")
            nc.vector.scalar_tensor_tensor(
                out=centred[:],
                in0=tiles["z", u][:],
                scalar=tiles["mean_var", u][:, 0:1],
                in1=everywhere["gamma"][:, m * PROJ : (m + 1) * PROJ],
                op0=ALU.subtract,
                op1=ALU.mult,
            )
            tiles["centred", u] = centred

        def inverse_root(name, u, column):
            root = small.tile([P, 1], F32, tag=name, name=name)
            nc.gpsimd.tensor_tensor(out=root[:], in0=column, in1=neg_half[:], op=ALU.pow)
            tiles[name, u] = root

        def inverse_root_scalar(name, u, column, bias):
            root = small.tile([P, 1], F32, tag=name, name=name)
            nc.scalar.activation(
                out=root[:], in_=column, func=ACT.Abs_reciprocal_sqrt, bias=bias
            )
            tiles[name, u] = root

        def inverse_deviation(u):
            var_eps = small.tile([P, 1], F32, tag="var_eps")
            nc.vector.tensor_scalar(
                out=var_eps[:],
                in0=tiles["mean_var", u][:, 1:2],
                scalar1=LN_EPS,
                scalar2=None,
                op0=ALU.add,
            )
            inverse_root("rstd", u, var_eps[:])

        def normalise(u):
            m = u // HALVES
            y = work.tile([P, PROJ], F32, tag="y")
            nc.vector.scalar_tensor_tensor(
                out=y[:],
                in0=tiles["centred", u][:],
                scalar=tiles["rstd", u][:],
                in1=everywhere["beta"][:, m * PROJ : (m + 1) * PROJ],
                op0=ALU.mult,
                op1=ALU.add,
            )
            tiles["y", u] = y

        def sum_squares(u):
            squares = work.tile([P, PROJ], F32, tag="squares")
            sum_sq = small.tile([P, 1], F32, tag="sum_sq")
            nc.scalar.activation(
                out=squares[:], in_=tiles["y", u][:], func=ACT.Square, accum_out=sum_sq[:]
            )
            tiles["sum_sq", u] = sum_sq

        def inverse_norm(u):
            floored = small.tile([P, 1], F32, tag="floored")
            nc.vector.tensor_scalar(
                out=floored[:],
                in0=tiles["sum_sq", u][:],
                scalar1=NORM_EPS * NORM_EPS,
                scalar2=None,
                op0=ALU.max,
            )
            inverse_root("rnorm", u, floored[:])

        def inverse_norm_scalar(u):
            excess = small.tile([P, 1], F32, tag="excess")
            nc.scalar.activation(
                out=excess[:], in_=tiles["sum_sq", u][:], func=ACT.Relu, bias=minus_eps2_col[:]
            )
            inverse_root_scalar("rnorm", u, excess[:], eps2_col[:])

        def finish(u):
            result = kept.tile([P, PROJ], F32, tag="result")
            nc.scalar.activation(
                out=result[:], in_=tiles["y", u][:], func=ACT.Copy, scale=tiles["rnorm", u][:]
            )
            tiles["result", u] = result

        def finish_on_vector(u):
            result = kept.tile([P, PROJ], F32, tag="result")
            nc.vector.tensor_scalar(
                out=result[:],
                in0=tiles["y", u][:],
                scalar1=tiles["rnorm", u][:],
                scalar2=None,
                op0=ALU.mult,
            )
            tiles["result", u] = result

        def store(queue, u):
            m, half = divmod(u, HALVES)
            queue.dma_start(out=out[m, half * P : (half + 1) * P, :], in_=tiles["result", u][:])

        def stage(work_of, u, *rest):
            if 0 <= u < UNITS:
                work_of(u, *rest)

        def both(work_of, u):
            if 0 <= u < UNITS:
                for n in range(PASSES):
                    work_of(u, n)

        def take_in(u, q):
            pool(u, q)
            round_mean(u, q)

        for u in range(UNITS):
            m, half = divmod(u, HALVES)
            take_in(u, 0)
            stage(inverse_norm, u - 3)
            both(first_matmul, u - 1)
            stage(second_matmul, u - 2)
            both(add_bias, u - 1)
            both(gelu, u - 1)
            stage(finish_on_vector, u - 3)
            stage(add_b2, u - 2)
            stage(centre, u - 2)
            stage(inverse_deviation, u - 2)
            take_in(u, 1)
            if u == 1:
                spread("beta", first_row["beta"], MODS * PROJ_TILES)
            take_in(u, 2)
            both(turn_h, u - 1)
            both(group_h, u - 1)
            both(quantise_h, u - 1)
            stage(normalise, u - 2)
            if u == 0:
                turn_vectors()
            take_in(u, 3)
            if u == 0:
                spread("b1_0", first_row["b1"], F_TILES)
                for name in ("b2", "gamma"):
                    spread(name, first_row[name], MODS * PROJ_TILES)
            if half == 1 and m + 1 < MODS:
                spread("b1_%d" % (m + 1), first_row["b1"] + (m + 1) * F_TILES, F_TILES)
            stage(sum_squares, u - 2)
            quantise_pooled(u)

        last = UNITS - 1
        both(first_matmul, last)
        second_matmul(last - 1)
        inverse_norm(last - 2)
        both(add_bias, last)
        both(gelu, last)
        finish_on_vector(last - 2)
        store(nc.sync, last - 2)
        for u in range(last - 2):
            store(nc.sync, u)
        add_b2(last - 1)
        inverse_deviation(last - 1)
        centre(last - 1)
        both(turn_h, last)
        both(group_h, last)
        both(quantise_h, last)
        nc.scalar.activation(out=warm[:], in_=eps_col[:], func=ACT.Abs_reciprocal_sqrt)
        normalise(last - 1)
        second_matmul(last)
        sum_squares(last - 1)
        add_b2(last)
        inverse_root_scalar("rstd", last, tiles["mean_var", last][:, 1:2], eps_col[:])
        centre(last)
        inverse_norm_scalar(last - 1)
        normalise(last)
        finish_on_vector(last - 1)
        store(nc.sync, last - 1)
        sum_squares(last)
        inverse_norm_scalar(last)
        finish(last)
        store(nc.sync, last)
